import numpy as np
import ml_dtypes


def mxq(x, axis, fmt="e4m3"):
    dtype, down = {"e4m3": (ml_dtypes.float8_e4m3fn, 7), "e5m2": (ml_dtypes.float8_e5m2, 14)}[fmt]
    v = np.moveaxis(np.asarray(x, np.float32).astype(ml_dtypes.bfloat16).astype(np.float64), axis, -1)
    blocks = v.reshape(v.shape[:-1] + (-1, 32))
    amax = np.abs(blocks).max(-1, keepdims=True)
    byte = np.maximum(np.where(amax > 0, np.frexp(amax)[1] - 1 + 127, 0) - down, 1)
    scale = np.exp2(byte - 127.0)
    codes = (blocks / scale).astype(np.float32).astype(dtype).astype(np.float64)
    return np.moveaxis((codes * scale).reshape(v.shape), -1, axis)


WIDE = False


def mx_kscale(k):
    if not WIDE:
        return np.ones(k)
    levels = np.array([10, -10, 5, -5, 0])
    a = np.random.permutation(np.resize(levels, k // 512 * 4)).reshape(k // 512, 4)
    idx = np.arange(k)
    return np.exp2(a[idx // 512, idx % 128 // 32])


BF16 = ml_dtypes.bfloat16


def bf(x):
    return np.asarray(x, np.float32).astype(BF16)


def f64(x):
    return np.asarray(x).astype(np.float64)


B, C, CK, H, W = 2, 1024, 512, 32, 32
N = H * W
EPS = 1e-5


def setup_inputs():
    s = mx_kscale(N)
    u = s / s.max()
    v = s.min() / s
    r = u.mean()
    fg0 = bf(np.random.uniform(size=(B, N, N)))
    return {
        "sim_fg": bf(np.random.standard_normal((B, N, N)) * f64(fg0)),
        "fg_sim": bf(f64(fg0) * u[None, None, :]),
        "bg_sim": bf(np.random.uniform(size=(B, N, N)) * 2.0 / N * u[None, None, :] / r),
        "x": bf(np.random.standard_normal((B, C, H, W)) * v.reshape(1, 1, H, W)),
        "gamma": bf(np.sqrt(N) * 0.3 * (1.0 + 0.1 * np.random.standard_normal(1)) * r * s.max() / s.min()),
    }


def reference(sim_fg, fg_sim, bg_sim, x, gamma):
    sim = f64(sim_fg)
    fg = f64(fg_sim)
    xf = f64(x).reshape(B, C, N)
    min_v = sim.min(-1, keepdims=True)
    x1 = (sim - min_v) * fg
    attn = x1 / (x1.sum(-1, keepdims=True) + EPS) + f64(bg_sim)
    value = xf.transpose(0, 2, 1)
    context = mxq(attn, 2, "e4m3") @ mxq(value, 1, "e4m3")
    context = context.transpose(0, 2, 1).reshape(B, C, H, W)
    return f64(gamma)[0] * context + f64(x)

@@ -1,0 +1,211 @@
+from contextlib import ExitStack
+
+import concourse.mybir as mybir
+from concourse.masks import make_identity
+
+F32 = mybir.dt.float32
+BF16 = mybir.dt.bfloat16
+U32 = mybir.dt.uint32
+U8 = mybir.dt.uint8
+FP8X4 = mybir.dt.float8_e4m3fn_x4
+ALU = mybir.AluOpType
+
+P = 128
+BATCH = 2
+PIXELS = 1024
+CHANNELS = 1024
+EPS = 1e-5
+PACK = 4
+K_PASS = P * PACK
+PASSES = PIXELS // K_PASS
+PLANES = 2
+UNIT = 512
+HALVES = PIXELS // UNIT
+ROW_TILES = UNIT // P
+PAIR = 2
+PAIRS = BATCH * HALVES * ROW_TILES // PAIR
+C_TILES = CHANNELS // P
+QUAD = 4
+AHEAD = 3
+
+FLOPS = 2 * BATCH * PIXELS * PIXELS * CHANNELS
+
+
+def tile_sgan_pb_kernel(tc, sim_fg, fg_sim, bg_sim, x, gamma, out):
+    nc = tc.nc
+
+    sim_rows = sim_fg.rearrange("b (h p j) m -> b h p j m", h=HALVES, j=ROW_TILES)
+    fg_rows = fg_sim.rearrange("b (h p j) m -> b h p j m", h=HALVES, j=ROW_TILES)
+    bg_rows = bg_sim.rearrange("b (h p j) m -> b h p j m", h=HALVES, j=ROW_TILES)
+    x_rows = x.rearrange("b (p t) r s -> b p t (r s)", t=C_TILES)
+    out_rows = out.rearrange("b (p t) r s -> b p t (r s)", t=C_TILES)
+
+    with ExitStack() as ctx:
+        const = ctx.enter_context(tc.tile_pool(name="const", bufs=1))
+        rows = ctx.enter_context(tc.tile_pool(name="rows", bufs=AHEAD + 1))
+        image = ctx.enter_context(tc.tile_pool(name="image", bufs=BATCH))
+        work = ctx.enter_context(tc.tile_pool(name="work", bufs=4))
+        stats = ctx.enter_context(tc.tile_pool(name="stats", bufs=3))
+        packed = ctx.enter_context(tc.tile_pool(name="packed", bufs=2))
+        turned = ctx.enter_context(tc.psum_pool(name="turned", bufs=4))
+        sums = ctx.enter_context(tc.psum_pool(name="sums", bufs=4))
+
+        identity = const.tile([P, P], F32, name="identity")
+        make_identity(nc, identity[:])
+        gamma_bf16 = const.tile([P, 1], BF16, name="gamma_bf16")
+        nc.scalar.dma_start(out=gamma_bf16[:], in_=gamma.partition_broadcast(P))
+        gamma_f32 = const.tile([P, 1], F32, name="gamma_f32")
+        nc.vector.tensor_copy(out=gamma_f32[:], in_=gamma_bf16[:])
+
+        def place(k):
+            b, rest = divmod(k, HALVES * ROW_TILES // PAIR)
+            h, q = divmod(rest, ROW_TILES // PAIR)
+            return b, h, q
+
+        def load_pair(k):
+            b, h, q = place(k)
+            js = slice(PAIR * q, PAIR * q + PAIR)
+            sim_t = rows.tile([P, PAIR, PIXELS], BF16, name="sim_t")
+            nc.sync.dma_start(out=sim_t[:], in_=sim_rows[b, h, :, js, :])
+            fg_t = rows.tile([P, PAIR, PIXELS], BF16, name="fg_t")
+            nc.sync.dma_start(out=fg_t[:], in_=fg_rows[b, h, :, js, :])
+            bg_t = rows.tile([P, PAIR, PIXELS], BF16, name="bg_t")
+            nc.sync.dma_start(out=bg_t[:], in_=bg_rows[b, h, :, js, :])
+            return sim_t, fg_t, bg_t
+
+        def load_channels(b, x_t, first):
+            for t in range(first, first + QUAD, PAIR):
+                nc.sync.dma_start(out=x_t[:, t : t + PAIR, :], in_=x_rows[b, :, t : t + PAIR, :])
+
+        def turn(source, grouped_words):
+            words = source.bitcast(F32)
+            bank = turned.tile([P, PASSES, PLANES, P], F32, name="bank")
+            for g in range(PASSES):
+                for u in range(PLANES):
+                    first = (g * PLANES + u) * P
+                    nc.tensor.transpose(bank[:, g, u, :], words[:, first : first + P], identity[:])
+            nc.scalar.copy(out=grouped_words, in_=bank[:].rearrange("k g u r -> k g r u"))
+
+        def normalise_pair(tiles, q, a_grouped):
+            sim_t, fg_t, bg_t = tiles
+            lowest = stats.tile([P, PAIR], F32, name="lowest")
+            total = stats.tile([P, PAIR], F32, name="total")
+            divisor = stats.tile([P, PAIR], F32, name="divisor")
+            inverse = stats.tile([P, PAIR], F32, name="inverse")
+            for i in range(PAIR):
+                unread = work.tile([P, PIXELS], BF16, name="unread", bufs=2)
+                nc.vector.tensor_scalar(
+                    out=unread[:],
+                    in0=sim_t[:, i, :],
+                    scalar1=1.0,
+                    scalar2=None,
+                    op0=ALU.mult,
+                    op1=ALU.min,
+                    accum_out=lowest[:, i : i + 1],
+                )
+            masked = []
+            for i in range(PAIR):
+                x1 = work.tile([P, PIXELS], F32, name="x1")
+                nc.vector.scalar_tensor_tensor(
+                    out=x1[:],
+                    in0=sim_t[:, i, :],
+                    scalar=lowest[:, i : i + 1],
+                    in1=fg_t[:, i, :],
+                    op0=ALU.subtract,
+                    op1=ALU.mult,
+                    accum_out=total[:, i : i + 1],
+                )
+                masked.append(x1)
+            nc.vector.tensor_scalar_add(out=divisor[:], in0=total[:], scalar1=EPS)
+            nc.vector.reciprocal(out=inverse[:], in_=divisor[:])
+            a_words = a_grouped[:].bitcast(F32)
+            for i in range(PAIR):
+                a_t = work.tile([P, PIXELS], BF16, name="a_t")
+                nc.vector.scalar_tensor_tensor(
+                    out=a_t[:],
+                    in0=masked[i][:],
+                    scalar=inverse[:, i : i + 1],
+                    in1=bg_t[:, i, :],
+                    op0=ALU.mult,
+                    op1=ALU.add,
+                )
+                first = (PAIR * q + i) * P
+                turn(a_t[:], a_words[:, :, first : first + P, :])
+
+        def quantise_channels(x_t, x_codes, x_scales):
+            for first in range(0, C_TILES, QUAD):
+                x_grouped = packed.tile([P, QUAD, PASSES, P, PACK], BF16, name="x_grouped", align_bytes=64)
+                x_words = x_grouped[:].bitcast(F32)
+                for i in range(QUAD):
+                    turn(x_t[:, first + i, :], x_words[:, i, :, :, :])
+                nc.vector.quantize_mx(
+                    out=x_codes[:, first : first + QUAD, :, :].rearrange("k t g c -> k (t g c)").bitcast(FP8X4),
+                    scales=x_scales[:, first : first + QUAD, :, :].rearrange("k t g c -> k (t g c)"),
+                    in_=x_grouped[:].rearrange("k t g c v -> k (t g c v)"),
+                )
+
+        def multiply_unit(b, h, a_grouped, x_t, x_codes, x_scales):
+            a_codes = packed.tile([P, PASSES, UNIT], U32, name="a_codes", align_bytes=64)
+            a_scales = packed.tile([P, PASSES, UNIT], U8, name="a_scales", align_bytes=64)
+            nc.vector.quantize_mx(
+                out=a_codes[:].rearrange("k g n -> k (g n)").bitcast(FP8X4),
+                scales=a_scales[:].rearrange("k g n -> k (g n)"),
+                in_=a_grouped[:].rearrange("k g n v -> k (g n v)"),
+            )
+            pixels = slice(h * UNIT, h * UNIT + UNIT)
+            for first in range(0, C_TILES, PAIR):
+                result = work.tile([P, PAIR, UNIT], F32, name="result")
+                for i in range(PAIR):
+                    t = first + i
+                    context = sums.tile([P, UNIT], F32, name="context")
+                    for g in range(PASSES):
+                        nc.tensor.matmul_mx(
+                            out=context[:],
+                            lhsT=x_codes[:, t, g, :].bitcast(FP8X4),
+                            lhsT_scale=x_scales[:, t, g, :],
+                            rhs=a_codes[:, g, :].bitcast(FP8X4),
+                            rhs_scale=a_scales[:, g, :],
+                            start=(g == 0),
+                            stop=(g == PASSES - 1),
+                        )
+                    nc.vector.scalar_tensor_tensor(
+                        out=result[:, i, :].rearrange("c (p j) -> c p j", j=ROW_TILES),
+                        in0=context[:].rearrange("c (j p) -> c p j", j=ROW_TILES),
+                        scalar=gamma_f32[:, 0:1],
+                        in1=x_t[:, t, pixels].rearrange("c (p j) -> c p j", j=ROW_TILES),
+                        op0=ALU.mult,
+                        op1=ALU.add,
+                    )
+                nc.sync.dma_start(out=out_rows[b, :, first : first + PAIR, pixels], in_=result[:])
+
+        loaded = {}
+        x_tiles = {}
+
+        def issue_loads(k):
+            if k >= PAIRS:
+                return
+            b, h, q = place(k)
+            loaded[k] = load_pair(k)
+            if h == 0:
+                if q == 0:
+                    x_tiles[b] = image.tile([P, C_TILES, PIXELS], BF16, name="x_t")
+                load_channels(b, x_tiles[b], q * QUAD)
+
+        for k in range(AHEAD):
+            issue_loads(k)
+
+        x_packed = {}
+        a_grouped = None
+        for k in range(PAIRS):
+            b, h, q = place(k)
+            issue_loads(k + AHEAD)
+            if q == 0:
+                a_grouped = packed.tile([P, PASSES, UNIT, PACK], BF16, name="a_grouped", align_bytes=64)
+            normalise_pair(loaded[k], q, a_grouped)
+            if h == 0 and q == 0:
+                x_codes = image.tile([P, C_TILES, PASSES, P], U32, name="x_codes", align_bytes=64)
+                x_scales = image.tile([P, C_TILES, PASSES, P], U8, name="x_scales", align_bytes=64)
+                quantise_channels(x_tiles[b], x_codes, x_scales)
+                x_packed[b] = (x_codes, x_scales)
+            if q == ROW_TILES // PAIR - 1:
+                multiply_unit(b, h, a_grouped, x_tiles[b], x_packed[b][0], x_packed[b][1])

@@ -9,6 +9,7 @@ U32 = mybir.dt.uint32
 U8 = mybir.dt.uint8
 FP8X4 = mybir.dt.float8_e4m3fn_x4
 ALU = mybir.AluOpType
+ACT = mybir.ActivationFunctionType
 
 P = 128
 BATCH = 2
@@ -86,6 +87,9 @@ def tile_sgan_pb_kernel(tc, sim_fg, fg_sim, bg_sim, x, gamma, out):
                     nc.tensor.transpose(bank[:, g, u, :], words[:, first : first + P], identity[:])
             nc.scalar.copy(out=grouped_words, in_=bank[:].rearrange("k g u r -> k g r u"))
 
+        def by_block(row):
+            return row.rearrange("n (w k e) -> n w e k", k=P, e=2)
+
         def normalise_pair(tiles, q, a_grouped):
             sim_t, fg_t, bg_t = tiles
             lowest = stats.tile([P, PAIR], F32, name="lowest")
@@ -118,19 +122,42 @@ def tile_sgan_pb_kernel(tc, sim_fg, fg_sim, bg_sim, x, gamma, out):
                 masked.append(x1)
             nc.vector.tensor_scalar_add(out=divisor[:], in0=total[:], scalar1=EPS)
             nc.vector.reciprocal(out=inverse[:], in_=divisor[:])
-            a_words = a_grouped[:].bitcast(F32)
             for i in range(PAIR):
-                a_t = work.tile([P, PIXELS], BF16, name="a_t")
-                nc.vector.scalar_tensor_tensor(
-                    out=a_t[:],
-                    in0=masked[i][:],
-                    scalar=inverse[:, i : i + 1],
-                    in1=bg_t[:, i, :],
-                    op0=ALU.mult,
-                    op1=ALU.add,
+                bg_f32 = work.tile([P, PASSES * PACK, P], F32, name="bg_f32")
+                nc.scalar.copy(
+                    out=bg_f32[:].rearrange("n (w e) k -> n w e k", e=2), in_=by_block(bg_t[:, i, :])
+                )
+                scaled = work.tile([P, PASSES * PACK, P], F32, name="scaled")
+                nc.scalar.activation(
+                    out=scaled[:].rearrange("n (w e) k -> n w e k", e=2),
+                    in_=by_block(masked[i][:]),
+                    func=ACT.Copy,
+                    scale=inverse[:, i : i + 1],
                 )
                 first = (PAIR * q + i) * P
-                turn(a_t[:], a_words[:, :, first : first + P, :])
+                for g in range(PASSES):
+                    bank = turned.tile([P, PACK, P], F32, name="bank")
+                    for t in range(PACK):
+                        block = g * PACK + t
+                        nc.tensor.matmul(
+                            out=bank[:, t, :],
+                            lhsT=scaled[:, block, :],
+                            rhs=identity[:],
+                            is_transpose=True,
+                            start=True,
+                            stop=False,
+                        )
+                        nc.tensor.matmul(
+                            out=bank[:, t, :],
+                            lhsT=bg_f32[:, block, :],
+                            rhs=identity[:],
+                            is_transpose=True,
+                            start=False,
+                            stop=True,
+                        )
+                    nc.scalar.copy(
+                        out=a_grouped[:, g, first : first + P, :], in_=bank[:].rearrange("k t r -> k r t")
+                    )
 
         def quantise_channels(x_t, x_codes, x_scales):
             for first in range(0, C_TILES, QUAD):

@@ -124,8 +124,13 @@ def tile_sgan_pb_kernel(tc, sim_fg, fg_sim, bg_sim, x, gamma, out):
             nc.vector.reciprocal(out=inverse[:], in_=divisor[:])
             for i in range(PAIR):
                 bg_f32 = work.tile([P, PASSES * PACK, P], F32, name="bg_f32")
-                nc.scalar.copy(
-                    out=bg_f32[:].rearrange("n (w e) k -> n w e k", e=2), in_=by_block(bg_t[:, i, :])
+                nc.gpsimd.tensor_scalar(
+                    out=bg_f32[:].rearrange("n (w e) k -> n w e k", e=2),
+                    in0=by_block(bg_t[:, i, :]),
+                    scalar1=1.0,
+                    scalar2=0.0,
+                    op0=ALU.mult,
+                    op1=ALU.add,
                 )
                 scaled = work.tile([P, PASSES * PACK, P], F32, name="scaled")
                 nc.scalar.activation(

@@ -23,11 +23,12 @@ PLANES = 2
 UNIT = 512
 HALVES = PIXELS // UNIT
 ROW_TILES = UNIT // P
+IMAGE_TILES = PIXELS // P
+TILES = BATCH * IMAGE_TILES
 PAIR = 2
-PAIRS = BATCH * HALVES * ROW_TILES // PAIR
-C_TILES = CHANNELS // P
-QUAD = 4
-AHEAD = 3
+GROUPS = TILES // PAIR
+AHEAD = 4
+LAG = ROW_TILES + 1
 
 FLOPS = 2 * BATCH * PIXELS * PIXELS * CHANNELS
 
@@ -35,209 +36,244 @@ FLOPS = 2 * BATCH * PIXELS * PIXELS * CHANNELS
 def tile_sgan_pb_kernel(tc, sim_fg, fg_sim, bg_sim, x, gamma, out):
     nc = tc.nc
 
-    sim_rows = sim_fg.rearrange("b (h p j) m -> b h p j m", h=HALVES, j=ROW_TILES)
-    fg_rows = fg_sim.rearrange("b (h p j) m -> b h p j m", h=HALVES, j=ROW_TILES)
-    bg_rows = bg_sim.rearrange("b (h p j) m -> b h p j m", h=HALVES, j=ROW_TILES)
-    x_rows = x.rearrange("b (p t) r s -> b p t (r s)", t=C_TILES)
-    out_rows = out.rearrange("b (p t) r s -> b p t (r s)", t=C_TILES)
+    sim_rows = sim_fg.rearrange("b (k i p) m -> (b k) p i m", i=PAIR, p=P)
+    fg_rows = fg_sim.rearrange("b (k i p) m -> (b k) p i m", i=PAIR, p=P)
+    bg_rows = bg_sim.rearrange("b (k i p) m -> (b k) p i m", i=PAIR, p=P)
+    x_rows = x.rearrange("b (p t) r s -> b p t (r s)", t=IMAGE_TILES)
+    out_rows = out.rearrange("b (p t) r s -> b p t (r s)", t=IMAGE_TILES)
 
     with ExitStack() as ctx:
         const = ctx.enter_context(tc.tile_pool(name="const", bufs=1))
         rows = ctx.enter_context(tc.tile_pool(name="rows", bufs=AHEAD + 1))
         image = ctx.enter_context(tc.tile_pool(name="image", bufs=BATCH))
-        work = ctx.enter_context(tc.tile_pool(name="work", bufs=4))
-        stats = ctx.enter_context(tc.tile_pool(name="stats", bufs=3))
+        work = ctx.enter_context(tc.tile_pool(name="work", bufs=3))
+        stats = ctx.enter_context(tc.tile_pool(name="stats", bufs=4))
         packed = ctx.enter_context(tc.tile_pool(name="packed", bufs=2))
-        turned = ctx.enter_context(tc.psum_pool(name="turned", bufs=4))
-        sums = ctx.enter_context(tc.psum_pool(name="sums", bufs=4))
+        a_banks = ctx.enter_context(tc.psum_pool(name="a_banks", bufs=4))
+        x_banks = ctx.enter_context(tc.psum_pool(name="x_banks", bufs=1))
+        sums = ctx.enter_context(tc.psum_pool(name="sums", bufs=3))
+        ctx.enter_context(tc.manual_schedule())
 
         identity = const.tile([P, P], F32, name="identity")
         make_identity(nc, identity[:])
-        gamma_bf16 = const.tile([P, 1], BF16, name="gamma_bf16")
-        nc.scalar.dma_start(out=gamma_bf16[:], in_=gamma.partition_broadcast(P))
-        gamma_f32 = const.tile([P, 1], F32, name="gamma_f32")
-        nc.vector.tensor_copy(out=gamma_f32[:], in_=gamma_bf16[:])
+        gamma_t = const.tile([P, 1], BF16, name="gamma_t")
+        nc.scalar.dma_start(out=gamma_t[:], in_=gamma.partition_broadcast(P))
 
-        def place(k):
-            b, rest = divmod(k, HALVES * ROW_TILES // PAIR)
-            h, q = divmod(rest, ROW_TILES // PAIR)
-            return b, h, q
+        sim_of, fg_of, bg_of = {}, {}, {}
+        lowest_of, x1_of, total_of, inverse_of = {}, {}, {}, {}
+        bg_f32_of, scaled_of, a_bank_of, x_bank_of = {}, {}, {}, {}
+        a_grouped_of, a_packed_of, x_grouped_of = {}, {}, {}
+        x_of, x_packed_of, context_of = {}, {}, {}
 
-        def load_pair(k):
-            b, h, q = place(k)
-            js = slice(PAIR * q, PAIR * q + PAIR)
-            sim_t = rows.tile([P, PAIR, PIXELS], BF16, name="sim_t")
-            nc.sync.dma_start(out=sim_t[:], in_=sim_rows[b, h, :, js, :])
-            fg_t = rows.tile([P, PAIR, PIXELS], BF16, name="fg_t")
-            nc.sync.dma_start(out=fg_t[:], in_=fg_rows[b, h, :, js, :])
-            bg_t = rows.tile([P, PAIR, PIXELS], BF16, name="bg_t")
-            nc.sync.dma_start(out=bg_t[:], in_=bg_rows[b, h, :, js, :])
-            return sim_t, fg_t, bg_t
+        def load_group(k):
+            for source, tiles, name in (
+                (sim_rows, sim_of, "sim_t"),
+                (fg_rows, fg_of, "fg_t"),
+                (bg_rows, bg_of, "bg_t"),
+            ):
+                pair_t = rows.tile([P, PAIR, PIXELS], BF16, name=name)
+                nc.sync.dma_start(out=pair_t[:], in_=source[k])
+                for i in range(PAIR):
+                    tiles[PAIR * k + i] = pair_t[:, i, :]
+            b, t = divmod(PAIR * k, IMAGE_TILES)
+            if t == 0:
+                x_of[b] = image.tile([P, IMAGE_TILES, PIXELS], BF16, name="x_t")
+            nc.sync.dma_start(out=x_of[b][:, t : t + PAIR, :], in_=x_rows[b, :, t : t + PAIR, :])
 
-        def load_channels(b, x_t, first):
-            for t in range(first, first + QUAD, PAIR):
-                nc.sync.dma_start(out=x_t[:, t : t + PAIR, :], in_=x_rows[b, :, t : t + PAIR, :])
+        def find_minimum(r):
+            unread = work.tile([P, PIXELS], BF16, name="unread")
+            lowest_of[r] = stats.tile([P, 1], F32, name="lowest")
+            nc.vector.tensor_scalar(
+                out=unread[:],
+                in0=sim_of[r],
+                scalar1=1.0,
+                scalar2=None,
+                op0=ALU.mult,
+                op1=ALU.min,
+                accum_out=lowest_of[r][:],
+            )
 
-        def turn(source, grouped_words):
-            words = source.bitcast(F32)
-            bank = turned.tile([P, PASSES, PLANES, P], F32, name="bank")
-            for g in range(PASSES):
-                for u in range(PLANES):
-                    first = (g * PLANES + u) * P
-                    nc.tensor.transpose(bank[:, g, u, :], words[:, first : first + P], identity[:])
-            nc.scalar.copy(out=grouped_words, in_=bank[:].rearrange("k g u r -> k g r u"))
+        def mask(r):
+            x1_of[r] = work.tile([P, PIXELS], F32, name="x1")
+            total_of[r] = stats.tile([P, 1], F32, name="total")
+            nc.vector.scalar_tensor_tensor(
+                out=x1_of[r][:],
+                in0=sim_of[r],
+                scalar=lowest_of[r][:],
+                in1=fg_of[r],
+                op0=ALU.subtract,
+                op1=ALU.mult,
+                accum_out=total_of[r][:],
+            )
+
+        def invert(r):
+            divisor = stats.tile([P, 1], F32, name="divisor")
+            nc.vector.tensor_scalar_add(out=divisor[:], in0=total_of[r][:], scalar1=EPS)
+            inverse_of[r] = stats.tile([P, 1], F32, name="inverse")
+            nc.vector.reciprocal(out=inverse_of[r][:], in_=divisor[:])
 
         def by_block(row):
             return row.rearrange("n (w k e) -> n w e k", k=P, e=2)
 
-        def normalise_pair(tiles, q, a_grouped):
-            sim_t, fg_t, bg_t = tiles
-            lowest = stats.tile([P, PAIR], F32, name="lowest")
-            total = stats.tile([P, PAIR], F32, name="total")
-            divisor = stats.tile([P, PAIR], F32, name="divisor")
-            inverse = stats.tile([P, PAIR], F32, name="inverse")
-            for i in range(PAIR):
-                unread = work.tile([P, PIXELS], BF16, name="unread", bufs=2)
-                nc.vector.tensor_scalar(
-                    out=unread[:],
-                    in0=sim_t[:, i, :],
-                    scalar1=1.0,
-                    scalar2=None,
-                    op0=ALU.mult,
-                    op1=ALU.min,
-                    accum_out=lowest[:, i : i + 1],
+        def blocks(tile_ap):
+            return tile_ap.rearrange("n (w e) k -> n w e k", e=2)
+
+        def widen_bg(r):
+            bg_f32_of[r] = work.tile([P, PASSES * PACK, P], F32, name="bg_f32")
+            nc.scalar.copy(out=blocks(bg_f32_of[r][:]), in_=by_block(bg_of[r]))
+
+        def scale(r):
+            scaled_of[r] = work.tile([P, PASSES * PACK, P], F32, name="scaled")
+            if r % 2 == 0:
+                nc.vector.tensor_scalar_mul(
+                    out=blocks(scaled_of[r][:]), in0=by_block(x1_of[r][:]), scalar1=inverse_of[r][:]
                 )
-            masked = []
-            for i in range(PAIR):
-                x1 = work.tile([P, PIXELS], F32, name="x1")
-                nc.vector.scalar_tensor_tensor(
-                    out=x1[:],
-                    in0=sim_t[:, i, :],
-                    scalar=lowest[:, i : i + 1],
-                    in1=fg_t[:, i, :],
-                    op0=ALU.subtract,
-                    op1=ALU.mult,
-                    accum_out=total[:, i : i + 1],
-                )
-                masked.append(x1)
-            nc.vector.tensor_scalar_add(out=divisor[:], in0=total[:], scalar1=EPS)
-            nc.vector.reciprocal(out=inverse[:], in_=divisor[:])
-            for i in range(PAIR):
-                bg_f32 = work.tile([P, PASSES * PACK, P], F32, name="bg_f32")
-                nc.gpsimd.tensor_scalar(
-                    out=bg_f32[:].rearrange("n (w e) k -> n w e k", e=2),
-                    in0=by_block(bg_t[:, i, :]),
-                    scalar1=1.0,
-                    scalar2=0.0,
-                    op0=ALU.mult,
-                    op1=ALU.add,
-                )
-                scaled = work.tile([P, PASSES * PACK, P], F32, name="scaled")
+            else:
                 nc.scalar.activation(
-                    out=scaled[:].rearrange("n (w e) k -> n w e k", e=2),
-                    in_=by_block(masked[i][:]),
+                    out=blocks(scaled_of[r][:]),
+                    in_=by_block(x1_of[r][:]),
                     func=ACT.Copy,
-                    scale=inverse[:, i : i + 1],
+                    scale=inverse_of[r][:],
                 )
-                first = (PAIR * q + i) * P
-                for g in range(PASSES):
-                    bank = turned.tile([P, PACK, P], F32, name="bank")
-                    for t in range(PACK):
-                        block = g * PACK + t
-                        nc.tensor.matmul(
-                            out=bank[:, t, :],
-                            lhsT=scaled[:, block, :],
-                            rhs=identity[:],
-                            is_transpose=True,
-                            start=True,
-                            stop=False,
-                        )
-                        nc.tensor.matmul(
-                            out=bank[:, t, :],
-                            lhsT=bg_f32[:, block, :],
-                            rhs=identity[:],
-                            is_transpose=True,
-                            start=False,
-                            stop=True,
-                        )
-                    nc.scalar.copy(
-                        out=a_grouped[:, g, first : first + P, :], in_=bank[:].rearrange("k t r -> k r t")
+
+        def turn_a(r):
+            a_bank_of[r] = []
+            for g in range(PASSES):
+                bank = a_banks.tile([P, PACK, P], F32, name="a_bank")
+                for t in range(PACK):
+                    block = g * PACK + t
+                    nc.tensor.matmul(
+                        out=bank[:, t, :],
+                        lhsT=scaled_of[r][:, block, :],
+                        rhs=identity[:],
+                        is_transpose=True,
+                        start=True,
+                        stop=False,
                     )
+                    nc.tensor.matmul(
+                        out=bank[:, t, :],
+                        lhsT=bg_f32_of[r][:, block, :],
+                        rhs=identity[:],
+                        is_transpose=True,
+                        start=False,
+                        stop=True,
+                    )
+                a_bank_of[r].append(bank)
 
-        def quantise_channels(x_t, x_codes, x_scales):
-            for first in range(0, C_TILES, QUAD):
-                x_grouped = packed.tile([P, QUAD, PASSES, P, PACK], BF16, name="x_grouped", align_bytes=64)
-                x_words = x_grouped[:].bitcast(F32)
-                for i in range(QUAD):
-                    turn(x_t[:, first + i, :], x_words[:, i, :, :, :])
-                nc.vector.quantize_mx(
-                    out=x_codes[:, first : first + QUAD, :, :].rearrange("k t g c -> k (t g c)").bitcast(FP8X4),
-                    scales=x_scales[:, first : first + QUAD, :, :].rearrange("k t g c -> k (t g c)"),
-                    in_=x_grouped[:].rearrange("k t g c v -> k (t g c v)"),
+        def group_a(r):
+            unit, j = divmod(r, ROW_TILES)
+            if j == 0:
+                a_grouped_of[unit] = packed.tile([P, PASSES, UNIT, PACK], BF16, name="a_grouped", align_bytes=64)
+            for g in range(PASSES):
+                nc.scalar.copy(
+                    out=a_grouped_of[unit][:, g, j * P : j * P + P, :],
+                    in_=a_bank_of[r][g][:].rearrange("k t n -> k n t"),
                 )
 
-        def multiply_unit(b, h, a_grouped, x_t, x_codes, x_scales):
+        def quantise_a(unit):
             a_codes = packed.tile([P, PASSES, UNIT], U32, name="a_codes", align_bytes=64)
             a_scales = packed.tile([P, PASSES, UNIT], U8, name="a_scales", align_bytes=64)
             nc.vector.quantize_mx(
                 out=a_codes[:].rearrange("k g n -> k (g n)").bitcast(FP8X4),
                 scales=a_scales[:].rearrange("k g n -> k (g n)"),
-                in_=a_grouped[:].rearrange("k g n v -> k (g n v)"),
+                in_=a_grouped_of[unit][:].rearrange("k g n v -> k (g n v)"),
             )
-            pixels = slice(h * UNIT, h * UNIT + UNIT)
-            for first in range(0, C_TILES, PAIR):
-                result = work.tile([P, PAIR, UNIT], F32, name="result")
-                for i in range(PAIR):
-                    t = first + i
-                    context = sums.tile([P, UNIT], F32, name="context")
-                    for g in range(PASSES):
-                        nc.tensor.matmul_mx(
-                            out=context[:],
-                            lhsT=x_codes[:, t, g, :].bitcast(FP8X4),
-                            lhsT_scale=x_scales[:, t, g, :],
-                            rhs=a_codes[:, g, :].bitcast(FP8X4),
-                            rhs_scale=a_scales[:, g, :],
-                            start=(g == 0),
-                            stop=(g == PASSES - 1),
-                        )
-                    nc.vector.scalar_tensor_tensor(
-                        out=result[:, i, :].rearrange("c (p j) -> c p j", j=ROW_TILES),
-                        in0=context[:].rearrange("c (j p) -> c p j", j=ROW_TILES),
-                        scalar=gamma_f32[:, 0:1],
-                        in1=x_t[:, t, pixels].rearrange("c (p j) -> c p j", j=ROW_TILES),
-                        op0=ALU.mult,
-                        op1=ALU.add,
+            a_packed_of[unit] = (a_codes, a_scales)
+
+        def turn_x(c):
+            b, t = divmod(c, IMAGE_TILES)
+            words = x_of[b][:, t, :].bitcast(F32)
+            x_bank_of[c] = x_banks.tile([P, PASSES, PLANES, P], F32, name="x_bank")
+            for g in range(PASSES):
+                for u in range(PLANES):
+                    first = (g * PLANES + u) * P
+                    nc.tensor.transpose(x_bank_of[c][:, g, u, :], words[:, first : first + P], identity[:])
+
+        def group_x(c):
+            pair, i = divmod(c, PAIR)
+            if i == 0:
+                x_grouped_of[pair] = packed.tile([P, PAIR, PASSES, P, PACK], BF16, name="x_grouped", align_bytes=64)
+            nc.scalar.copy(
+                out=x_grouped_of[pair][:].bitcast(F32)[:, i, :, :, :],
+                in_=x_bank_of[c][:].rearrange("k g u c -> k g c u"),
+            )
+
+        def quantise_x(pair):
+            b, t = divmod(PAIR * pair, IMAGE_TILES)
+            if t == 0:
+                x_codes = image.tile([P, IMAGE_TILES, PASSES, P], U32, name="x_codes", align_bytes=64)
+                x_scales = image.tile([P, IMAGE_TILES, PASSES, P], U8, name="x_scales", align_bytes=64)
+                x_packed_of[b] = (x_codes, x_scales)
+            x_codes, x_scales = x_packed_of[b]
+            nc.vector.quantize_mx(
+                out=x_codes[:, t : t + PAIR, :, :].rearrange("k t g c -> k (t g c)").bitcast(FP8X4),
+                scales=x_scales[:, t : t + PAIR, :, :].rearrange("k t g c -> k (t g c)"),
+                in_=x_grouped_of[pair][:].rearrange("k t g c v -> k (t g c v)"),
+            )
+
+        def multiply(unit, pair):
+            a_codes, a_scales = a_packed_of[unit]
+            x_codes, x_scales = x_packed_of[unit // HALVES]
+            for i in range(PAIR):
+                t = PAIR * pair + i
+                context = sums.tile([P, UNIT], F32, name="context")
+                for g in range(PASSES):
+                    nc.tensor.matmul_mx(
+                        out=context[:],
+                        lhsT=x_codes[:, t, g, :].bitcast(FP8X4),
+                        lhsT_scale=x_scales[:, t, g, :],
+                        rhs=a_codes[:, g, :].bitcast(FP8X4),
+                        rhs_scale=a_scales[:, g, :],
+                        start=(g == 0),
+                        stop=(g == PASSES - 1),
                     )
-                nc.sync.dma_start(out=out_rows[b, :, first : first + PAIR, pixels], in_=result[:])
+                context_of[(unit, t)] = context
 
-        loaded = {}
-        x_tiles = {}
-
-        def issue_loads(k):
-            if k >= PAIRS:
-                return
-            b, h, q = place(k)
-            loaded[k] = load_pair(k)
-            if h == 0:
-                if q == 0:
-                    x_tiles[b] = image.tile([P, C_TILES, PIXELS], BF16, name="x_t")
-                load_channels(b, x_tiles[b], q * QUAD)
+        def finish(unit, pair):
+            b, h = divmod(unit, HALVES)
+            pixels = slice(h * UNIT, h * UNIT + UNIT)
+            first = PAIR * pair
+            result = work.tile([P, PAIR, UNIT], F32, name="result")
+            for i in range(PAIR):
+                nc.vector.scalar_tensor_tensor(
+                    out=result[:, i, :],
+                    in0=context_of[(unit, first + i)][:],
+                    scalar=gamma_t[:, 0:1],
+                    in1=x_of[b][:, first + i, pixels],
+                    op0=ALU.mult,
+                    op1=ALU.add,
+                )
+            nc.sync.dma_start(out=out_rows[b, :, first : first + PAIR, pixels], in_=result[:])
 
         for k in range(AHEAD):
-            issue_loads(k)
-
-        x_packed = {}
-        a_grouped = None
-        for k in range(PAIRS):
-            b, h, q = place(k)
-            issue_loads(k + AHEAD)
-            if q == 0:
-                a_grouped = packed.tile([P, PASSES, UNIT, PACK], BF16, name="a_grouped", align_bytes=64)
-            normalise_pair(loaded[k], q, a_grouped)
-            if h == 0 and q == 0:
-                x_codes = image.tile([P, C_TILES, PASSES, P], U32, name="x_codes", align_bytes=64)
-                x_scales = image.tile([P, C_TILES, PASSES, P], U8, name="x_scales", align_bytes=64)
-                quantise_channels(x_tiles[b], x_codes, x_scales)
-                x_packed[b] = (x_codes, x_scales)
-            if q == ROW_TILES // PAIR - 1:
-                multiply_unit(b, h, a_grouped, x_tiles[b], x_packed[b][0], x_packed[b][1])
+            load_group(k)
+        find_minimum(0)
+        widen_bg(0)
+        for step in range(TILES + LAG):
+            rows_left = step < TILES
+            if step % PAIR == 0 and step // PAIR + AHEAD < GROUPS:
+                load_group(step // PAIR + AHEAD)
+            if rows_left:
+                turn_x(step)
+            if step >= LAG:
+                multiply((step - LAG) // ROW_TILES, (step - LAG) % ROW_TILES)
+            if rows_left:
+                mask(step)
+            if step + 1 < TILES:
+                find_minimum(step + 1)
+                widen_bg(step + 1)
+            if rows_left:
+                invert(step)
+            if 1 <= step <= TILES:
+                group_a(step - 1)
+            if rows_left:
+                group_x(step)
+                scale(step)
+            if step >= LAG:
+                finish((step - LAG) // ROW_TILES, (step - LAG) % ROW_TILES)
+            if rows_left:
+                turn_a(step)
+            if 1 <= step <= TILES and step % ROW_TILES == 0:
+                quantise_a(step // ROW_TILES - 1)
+            if rows_left and step % PAIR == 1:
+                quantise_x(step // PAIR)

from contextlib import ExitStack

import concourse.mybir as mybir
from concourse.masks import make_identity

F32 = mybir.dt.float32
BF16 = mybir.dt.bfloat16
U32 = mybir.dt.uint32
U8 = mybir.dt.uint8
FP8X4 = mybir.dt.float8_e4m3fn_x4
ALU = mybir.AluOpType
ACT = mybir.ActivationFunctionType

P = 128
BATCH = 2
PIXELS = 1024
CHANNELS = 1024
EPS = 1e-5
PACK = 4
K_PASS = P * PACK
PASSES = PIXELS // K_PASS
PLANES = 2
UNIT = 512
HALVES = PIXELS // UNIT
ROW_TILES = UNIT // P
IMAGE_TILES = PIXELS // P
TILES = BATCH * IMAGE_TILES
PAIR = 2
GROUPS = TILES // PAIR
AHEAD = 4
LAG = ROW_TILES + 1

FLOPS = 2 * BATCH * PIXELS * PIXELS * CHANNELS


def tile_sgan_pb_kernel(tc, sim_fg, fg_sim, bg_sim, x, gamma, out):
    nc = tc.nc

    sim_rows = sim_fg.rearrange("b (k i p) m -> (b k) p i m", i=PAIR, p=P)
    fg_rows = fg_sim.rearrange("b (k i p) m -> (b k) p i m", i=PAIR, p=P)
    bg_rows = bg_sim.rearrange("b (k i p) m -> (b k) p i m", i=PAIR, p=P)
    x_rows = x.rearrange("b (p t) r s -> b p t (r s)", t=IMAGE_TILES)
    out_rows = out.rearrange("b (p t) r s -> b p t (r s)", t=IMAGE_TILES)

    with ExitStack() as ctx:
        const = ctx.enter_context(tc.tile_pool(name="const", bufs=1))
        rows = ctx.enter_context(tc.tile_pool(name="rows", bufs=AHEAD + 1))
        image = ctx.enter_context(tc.tile_pool(name="image", bufs=BATCH))
        work = ctx.enter_context(tc.tile_pool(name="work", bufs=3))
        stats = ctx.enter_context(tc.tile_pool(name="stats", bufs=4))
        packed = ctx.enter_context(tc.tile_pool(name="packed", bufs=2))
        a_banks = ctx.enter_context(tc.psum_pool(name="a_banks", bufs=4))
        x_banks = ctx.enter_context(tc.psum_pool(name="x_banks", bufs=1))
        sums = ctx.enter_context(tc.psum_pool(name="sums", bufs=3))
        ctx.enter_context(tc.manual_schedule())

        identity = const.tile([P, P], F32, name="identity")
        make_identity(nc, identity[:])
        gamma_t = const.tile([P, 1], BF16, name="gamma_t")
        nc.scalar.dma_start(out=gamma_t[:], in_=gamma.partition_broadcast(P))

        sim_of, fg_of, bg_of = {}, {}, {}
        lowest_of, x1_of, total_of, inverse_of = {}, {}, {}, {}
        bg_f32_of, scaled_of, a_bank_of, x_bank_of = {}, {}, {}, {}
        a_grouped_of, a_packed_of, x_grouped_of = {}, {}, {}
        x_of, x_packed_of, context_of = {}, {}, {}

        def load_group(k):
            for source, tiles, name in (
                (sim_rows, sim_of, "sim_t"),
                (fg_rows, fg_of, "fg_t"),
                (bg_rows, bg_of, "bg_t"),
            ):
                pair_t = rows.tile([P, PAIR, PIXELS], BF16, name=name)
                nc.sync.dma_start(out=pair_t[:], in_=source[k])
                for i in range(PAIR):
                    tiles[PAIR * k + i] = pair_t[:, i, :]
            b, t = divmod(PAIR * k, IMAGE_TILES)
            if t == 0:
                x_of[b] = image.tile([P, IMAGE_TILES, PIXELS], BF16, name="x_t")
            nc.sync.dma_start(out=x_of[b][:, t : t + PAIR, :], in_=x_rows[b, :, t : t + PAIR, :])

        def find_minimum(r):
            unread = work.tile([P, PIXELS], BF16, name="unread")
            lowest_of[r] = stats.tile([P, 1], F32, name="lowest")
            nc.vector.tensor_scalar(
                out=unread[:],
                in0=sim_of[r],
                scalar1=1.0,
                scalar2=None,
                op0=ALU.mult,
                op1=ALU.min,
                accum_out=lowest_of[r][:],
            )

        def mask(r):
            x1_of[r] = work.tile([P, PIXELS], F32, name="x1")
            total_of[r] = stats.tile([P, 1], F32, name="total")
            nc.vector.scalar_tensor_tensor(
                out=x1_of[r][:],
                in0=sim_of[r],
                scalar=lowest_of[r][:],
                in1=fg_of[r],
                op0=ALU.subtract,
                op1=ALU.mult,
                accum_out=total_of[r][:],
            )

        def invert(r):
            divisor = stats.tile([P, 1], F32, name="divisor")
            nc.vector.tensor_scalar_add(out=divisor[:], in0=total_of[r][:], scalar1=EPS)
            inverse_of[r] = stats.tile([P, 1], F32, name="inverse")
            nc.vector.reciprocal(out=inverse_of[r][:], in_=divisor[:])

        def by_block(row):
            return row.rearrange("n (w k e) -> n w e k", k=P, e=2)

        def blocks(tile_ap):
            return tile_ap.rearrange("n (w e) k -> n w e k", e=2)

        def widen_bg(r):
            bg_f32_of[r] = work.tile([P, PASSES * PACK, P], F32, name="bg_f32")
            nc.scalar.copy(out=blocks(bg_f32_of[r][:]), in_=by_block(bg_of[r]))

        def scale(r):
            scaled_of[r] = work.tile([P, PASSES * PACK, P], F32, name="scaled")
            if r % 2 == 0:
                nc.vector.tensor_scalar_mul(
                    out=blocks(scaled_of[r][:]), in0=by_block(x1_of[r][:]), scalar1=inverse_of[r][:]
                )
            else:
                nc.scalar.activation(
                    out=blocks(scaled_of[r][:]),
                    in_=by_block(x1_of[r][:]),
                    func=ACT.Copy,
                    scale=inverse_of[r][:],
                )

        def turn_a(r):
            a_bank_of[r] = []
            for g in range(PASSES):
                bank = a_banks.tile([P, PACK, P], F32, name="a_bank")
                for t in range(PACK):
                    block = g * PACK + t
                    nc.tensor.matmul(
                        out=bank[:, t, :],
                        lhsT=scaled_of[r][:, block, :],
                        rhs=identity[:],
                        is_transpose=True,
                        start=True,
                        stop=False,
                    )
                    nc.tensor.matmul(
                        out=bank[:, t, :],
                        lhsT=bg_f32_of[r][:, block, :],
                        rhs=identity[:],
                        is_transpose=True,
                        start=False,
                        stop=True,
                    )
                a_bank_of[r].append(bank)

        def group_a(r):
            unit, j = divmod(r, ROW_TILES)
            if j == 0:
                a_grouped_of[unit] = packed.tile([P, PASSES, UNIT, PACK], BF16, name="a_grouped", align_bytes=64)
            for g in range(PASSES):
                nc.scalar.copy(
                    out=a_grouped_of[unit][:, g, j * P : j * P + P, :],
                    in_=a_bank_of[r][g][:].rearrange("k t n -> k n t"),
                )

        def quantise_a(unit):
            a_codes = packed.tile([P, PASSES, UNIT], U32, name="a_codes", align_bytes=64)
            a_scales = packed.tile([P, PASSES, UNIT], U8, name="a_scales", align_bytes=64)
            nc.vector.quantize_mx(
                out=a_codes[:].rearrange("k g n -> k (g n)").bitcast(FP8X4),
                scales=a_scales[:].rearrange("k g n -> k (g n)"),
                in_=a_grouped_of[unit][:].rearrange("k g n v -> k (g n v)"),
            )
            a_packed_of[unit] = (a_codes, a_scales)

        def turn_x(c):
            b, t = divmod(c, IMAGE_TILES)
            words = x_of[b][:, t, :].bitcast(F32)
            x_bank_of[c] = x_banks.tile([P, PASSES, PLANES, P], F32, name="x_bank")
            for g in range(PASSES):
                for u in range(PLANES):
                    first = (g * PLANES + u) * P
                    nc.tensor.transpose(x_bank_of[c][:, g, u, :], words[:, first : first + P], identity[:])

        def group_x(c):
            pair, i = divmod(c, PAIR)
            if i == 0:
                x_grouped_of[pair] = packed.tile([P, PAIR, PASSES, P, PACK], BF16, name="x_grouped", align_bytes=64)
            nc.scalar.copy(
                out=x_grouped_of[pair][:].bitcast(F32)[:, i, :, :, :],
                in_=x_bank_of[c][:].rearrange("k g u c -> k g c u"),
            )

        def quantise_x(pair):
            b, t = divmod(PAIR * pair, IMAGE_TILES)
            if t == 0:
                x_codes = image.tile([P, IMAGE_TILES, PASSES, P], U32, name="x_codes", align_bytes=64)
                x_scales = image.tile([P, IMAGE_TILES, PASSES, P], U8, name="x_scales", align_bytes=64)
                x_packed_of[b] = (x_codes, x_scales)
            x_codes, x_scales = x_packed_of[b]
            nc.vector.quantize_mx(
                out=x_codes[:, t : t + PAIR, :, :].rearrange("k t g c -> k (t g c)").bitcast(FP8X4),
                scales=x_scales[:, t : t + PAIR, :, :].rearrange("k t g c -> k (t g c)"),
                in_=x_grouped_of[pair][:].rearrange("k t g c v -> k (t g c v)"),
            )

        def multiply(unit, pair):
            a_codes, a_scales = a_packed_of[unit]
            x_codes, x_scales = x_packed_of[unit // HALVES]
            for i in range(PAIR):
                t = PAIR * pair + i
                context = sums.tile([P, UNIT], F32, name="context")
                for g in range(PASSES):
                    nc.tensor.matmul_mx(
                        out=context[:],
                        lhsT=x_codes[:, t, g, :].bitcast(FP8X4),
                        lhsT_scale=x_scales[:, t, g, :],
                        rhs=a_codes[:, g, :].bitcast(FP8X4),
                        rhs_scale=a_scales[:, g, :],
                        start=(g == 0),
                        stop=(g == PASSES - 1),
                    )
                context_of[(unit, t)] = context

        def finish(unit, pair):
            b, h = divmod(unit, HALVES)
            pixels = slice(h * UNIT, h * UNIT + UNIT)
            first = PAIR * pair
            result = work.tile([P, PAIR, UNIT], F32, name="result")
            for i in range(PAIR):
                nc.vector.scalar_tensor_tensor(
                    out=result[:, i, :],
                    in0=context_of[(unit, first + i)][:],
                    scalar=gamma_t[:, 0:1],
                    in1=x_of[b][:, first + i, pixels],
                    op0=ALU.mult,
                    op1=ALU.add,
                )
            nc.sync.dma_start(out=out_rows[b, :, first : first + PAIR, pixels], in_=result[:])

        for k in range(AHEAD):
            load_group(k)
        find_minimum(0)
        widen_bg(0)
        for step in range(TILES + LAG):
            rows_left = step < TILES
            if step % PAIR == 0 and step // PAIR + AHEAD < GROUPS:
                load_group(step // PAIR + AHEAD)
            if rows_left:
                turn_x(step)
            if step >= LAG:
                multiply((step - LAG) // ROW_TILES, (step - LAG) % ROW_TILES)
            if rows_left:
                mask(step)
            if step + 1 < TILES:
                find_minimum(step + 1)
                widen_bg(step + 1)
            if rows_left:
                invert(step)
            if 1 <= step <= TILES:
                group_a(step - 1)
            if rows_left:
                group_x(step)
                scale(step)
            if step >= LAG:
                finish((step - LAG) // ROW_TILES, (step - LAG) % ROW_TILES)
            if rows_left:
                turn_a(step)
            if 1 <= step <= TILES and step % ROW_TILES == 0:
                quantise_a(step // ROW_TILES - 1)
            if rows_left and step % PAIR == 1:
                quantise_x(step // PAIR)
